import numpy as np
import ml_dtypes


def mxq(x, axis, fmt="e4m3"):
    dtype, down = {"e4m3": (ml_dtypes.float8_e4m3fn, 7), "e5m2": (ml_dtypes.float8_e5m2, 14)}[fmt]
    v = np.moveaxis(np.asarray(x, np.float32).astype(ml_dtypes.bfloat16).astype(np.float64), axis, -1)
    blocks = v.reshape(v.shape[:-1] + (-1, 32))
    amax = np.abs(blocks).max(-1, keepdims=True)
    byte = np.maximum(np.where(amax > 0, np.frexp(amax)[1] - 1 + 127, 0) - down, 1)
    scale = np.exp2(byte - 127.0)
    codes = (blocks / scale).astype(np.float32).astype(dtype).astype(np.float64)
    return np.moveaxis((codes * scale).reshape(v.shape), -1, axis)


WIDE = False


def mx_kscale(k):
    if not WIDE:
        return np.ones(k)
    levels = np.array([10, -10, 5, -5, 0])
    if k % 512:
        return np.exp2(np.random.permutation(np.resize(levels, k // 32))).repeat(32)
    a = np.empty((k // 512, 16))
    for p in range(k // 512):
        a[p, :8] = np.random.permutation(np.resize(levels, 8))
        for g in range(8):
            far = levels[np.abs(levels - a[p, g]) >= 10]
            a[p, g + 8] = far[np.random.randint(len(far))]
    return np.exp2(a.ravel()).repeat(32)


BF16 = ml_dtypes.bfloat16


def bf(x):
    return np.asarray(x, np.float32).astype(BF16)


def f64(x):
    return np.asarray(x).astype(np.float64)


B, D, MP, MID, L = 1024, 768, 1024, 1024, 4
HALF = D // 2


def setup_inputs():
    s = mx_kscale(MP)
    t = mx_kscale(MID)
    return {
        "x": bf(np.random.standard_normal((B, D))),
        "h_prev": bf(np.maximum(np.random.standard_normal((B, MP)) * np.sqrt(2.0), 0.0) * s),
        "w_hid": bf(np.random.standard_normal((MP, MID)) * np.sqrt(2.0 / MP) / s[:, None] * t),
        "b_hid": bf(np.random.standard_normal(MID) * 0.2 * t),
        "w_out": bf(np.random.standard_normal((MID, HALF)) / np.sqrt(MID) / t[:, None]),
        "b_out": bf(np.random.standard_normal(HALF) * 0.2),
    }


def reference(x, h_prev, w_hid, b_hid, w_out, b_out):
    x = f64(x)
    first = x[:, 0::2]
    second = x[:, 1::2]
    h = np.maximum((mxq(f64(h_prev), 1, "e4m3") @ mxq(f64(w_hid), 0, "e4m3")) + f64(b_hid), 0.0)
    shift = (mxq(h, 1, "e4m3") @ mxq(f64(w_out), 0, "e4m3")) + f64(b_out)
    y_second = second + shift
    return np.stack([first, y_second], axis=2).reshape(x.shape)

@@ -1,0 +1,304 @@
+from contextlib import ExitStack
+
+import concourse.mybir as mybir
+from concourse.masks import make_identity
+
+F32 = mybir.dt.float32
+BF16 = mybir.dt.bfloat16
+U32 = mybir.dt.uint32
+U8 = mybir.dt.uint8
+FP8X4 = mybir.dt.float8_e4m3fn_x4
+ADD = mybir.AluOpType.add
+RELU = mybir.ActivationFunctionType.Relu
+IDENTITY = mybir.ActivationFunctionType.Identity
+
+P = 128
+PACK = 4
+K_PASS = P * PACK
+B, D, MP, MID = 1024, 768, 1024, 1024
+HALF = D // 2
+B_TILES = B // P
+B_HALF = 512
+PASSES = MP // K_PASS
+J_TILES = HALF // P
+Y_BANKS = 4
+W_PIECE = 256
+
+FLOPS = 2 * B * MP * MID + 2 * B * MID * HALF
+
+
+def tile_additivecoupling_pa_kernel(tc, x, h_prev, w_hid, b_hid, w_out, b_out, out):
+    nc = tc.nc
+    with ExitStack() as ctx:
+        keep = ctx.enter_context(tc.tile_pool(name="keep", bufs=1))
+        y_pool = ctx.enter_context(tc.tile_pool(name="y_pool", bufs=12))
+        psum_acc = ctx.enter_context(tc.psum_pool(name="psum_acc", bufs=4))
+        psum_y = ctx.enter_context(tc.psum_pool(name="psum_y", bufs=1))
+
+        hp_rows = keep.tile([P, B_TILES, MP], BF16)
+        hp_grouped = keep.tile([P, PASSES, B * PACK], BF16, align_bytes=64)
+        hp_codes = keep.tile([P, PASSES, B], U32, align_bytes=64)
+        hp_scales = keep.tile([P, PASSES, B], U8, align_bytes=64)
+
+        w_raw = keep.tile([P, 2, PASSES, PACK, 512], BF16)
+        w_grouped = keep.tile([P, 2, PASSES, 512 * PACK], BF16, align_bytes=64)
+        w_codes = keep.tile([P, PASSES, MID], U32, align_bytes=64)
+        w_scales = keep.tile([P, PASSES, MID], U8, align_bytes=64)
+
+        h_rows = keep.tile([P, PASSES, PACK, B], BF16)
+        h_grouped = keep.tile([P, PASSES, B * PACK], BF16, align_bytes=64)
+        h_codes = keep.tile([P, PASSES, B], U32, align_bytes=64)
+        h_scales = keep.tile([P, PASSES, B], U8, align_bytes=64)
+
+        wo_raw = keep.tile([P, PASSES, PACK, HALF], BF16)
+        wo_grouped = keep.tile([P, PASSES * HALF * PACK], BF16, align_bytes=64)
+        wo_codes = keep.tile([P, PASSES * HALF], U32, align_bytes=64)
+        wo_scales = keep.tile([P, PASSES * HALF], U8, align_bytes=64)
+
+        x_rows = keep.tile([P, B_TILES, D], BF16)
+        shift_t = keep.tile([P, J_TILES, B], F32)
+
+        ident_f32 = keep.tile([P, P], F32)
+        ident_bf16 = keep.tile([P, P], BF16)
+        zeros_f32 = keep.tile([P, P], F32)
+        bias_rows = keep.tile([P, P], BF16)
+        bias_hid = keep.tile([P, PASSES, PACK], BF16)
+        bias_out = keep.tile([P, J_TILES], F32)
+
+        y_banks = [psum_y.tile([P, 4, P], F32, name="y_bank%d" % i) for i in range(Y_BANKS)]
+
+        nc.vector.memset(bias_rows[:], 0.0)
+        nc.vector.memset(zeros_f32[:], 0.0)
+        nc.scalar.dma_start(out=bias_rows[0:J_TILES, :], in_=b_out.rearrange("(m p) -> m p", p=P))
+        nc.scalar.dma_start(out=bias_hid[:], in_=b_hid.rearrange("(g p t) -> p g t", p=P, t=PACK))
+
+        def load_h_prev(duo):
+            nc.sync.dma_start(
+                out=hp_rows[:, 2 * duo : 2 * duo + 2, :],
+                in_=h_prev[2 * P * duo : 2 * P * (duo + 1), :].rearrange("(p k) c -> p k c", k=2),
+            )
+
+        def load_w_hid(mh):
+            for g in range(PASSES):
+                nc.sync.dma_start(
+                    out=w_raw[:, mh, g, :, :],
+                    in_=w_hid[K_PASS * g : K_PASS * (g + 1), 512 * mh : 512 * mh + 512].rearrange(
+                        "(p t) c -> p t c", t=PACK
+                    ),
+                )
+
+        load_w_hid(0)
+        for duo in range(2):
+            load_h_prev(duo)
+        nc.sync.dma_start(
+            out=wo_raw[:].rearrange("p g t n -> p g (t n)"),
+            in_=w_out.rearrange("(g p t) n -> p g (t n)", p=P, t=PACK),
+        )
+        for duo in range(2, 4):
+            load_h_prev(duo)
+        load_w_hid(1)
+        for xh in range(2):
+            nc.sync.dma_start(
+                out=x_rows[:, 4 * xh : 4 * xh + 4, :].rearrange("p (c k) d -> p c (k d)", k=2),
+                in_=x[B_HALF * xh : B_HALF * (xh + 1), :].rearrange("(c p k) d -> p c (k d)", p=P, k=2),
+            )
+
+        make_identity(nc, ident_f32[:])
+        nc.vector.tensor_copy(out=ident_bf16[:], in_=ident_f32[:])
+
+        def spread_biases():
+            bias_t = psum_acc.tile([P, P], BF16, tag="acc")
+            nc.tensor.transpose(bias_t[:], bias_rows[:], ident_bf16[:])
+            nc.vector.tensor_copy(out=bias_out[:], in_=bias_t[:, 0:J_TILES])
+            for bank in y_banks:
+                for k in range(2):
+                    nc.tensor.transpose(bank[:, 2 * k, :], zeros_f32[:], ident_f32[:])
+
+        def transpose_h_prev(bt):
+            words = hp_rows[:, bt, :].bitcast(F32)
+            pairs_t = psum_acc.tile([P, 2 * PASSES, P], F32, tag="acc")
+            for g in range(PASSES):
+                for u in range(2):
+                    nc.tensor.transpose(
+                        pairs_t[:, 2 * g + u, :], words[:, 2 * P * g + u : 2 * P * (g + 1) : 2], ident_f32[:]
+                    )
+            nc.scalar.copy(
+                out=hp_grouped[:, :, bt * P * PACK : (bt + 1) * P * PACK]
+                .bitcast(F32)
+                .rearrange("q g (b u) -> q g b u", u=2),
+                in_=pairs_t[:].rearrange("q (g u) b -> q g b u", u=2),
+            )
+
+        def quantise_h_prev(pair):
+            cols = slice(pair * 2 * P, (pair + 1) * 2 * P)
+            wide = slice(pair * 2 * P * PACK, (pair + 1) * 2 * P * PACK)
+            for g in range(PASSES):
+                nc.vector.quantize_mx(
+                    out=hp_codes[:, g, cols].bitcast(FP8X4), scales=hp_scales[:, g, cols], in_=hp_grouped[:, g, wide]
+                )
+
+        def regroup(dst, src):
+            nc.vector.tensor_copy(
+                out=dst.rearrange("p (c i) t -> p c t i", i=4),
+                in_=src.rearrange("p t (c i) -> p c t i", i=4),
+            )
+
+        def prepare_w_hid(mh):
+            for piece in range(512 // W_PIECE):
+                c0 = piece * W_PIECE
+                for g in range(PASSES):
+                    nc.vector.tensor_copy(
+                        out=w_grouped[:, mh, g, c0 * PACK : (c0 + W_PIECE) * PACK].rearrange(
+                            "p (t m j) -> p t m j", t=2, j=PACK
+                        ),
+                        in_=w_raw[:, mh, g, :, :].rearrange("p j (m t) -> p t m j", t=PACK)[
+                            :, 2 * piece : 2 * piece + 2, :, :
+                        ],
+                    )
+                for g in range(PASSES):
+                    nc.vector.quantize_mx(
+                        out=w_codes[:, g, 512 * mh + c0 : 512 * mh + c0 + W_PIECE].bitcast(FP8X4),
+                        scales=w_scales[:, g, 512 * mh + c0 : 512 * mh + c0 + W_PIECE],
+                        in_=w_grouped[:, mh, g, c0 * PACK : (c0 + W_PIECE) * PACK],
+                    )
+
+        def hidden_matmuls(mh, bh):
+            cols = slice(bh * B_HALF, (bh + 1) * B_HALF)
+            for t in range(PACK):
+                mt = PACK * mh + t
+                acc = psum_acc.tile([P, B_HALF], F32, tag="acc")
+                for g in range(PASSES):
+                    nc.tensor.matmul_mx(
+                        out=acc[:],
+                        lhsT=w_codes[:, g, mt * P : (mt + 1) * P].bitcast(FP8X4),
+                        lhsT_scale=w_scales[:, g, mt * P : (mt + 1) * P],
+                        rhs=hp_codes[:, g, cols].bitcast(FP8X4),
+                        rhs_scale=hp_scales[:, g, cols],
+                        start=(g == 0),
+                        stop=(g == PASSES - 1),
+                    )
+                nc.scalar.activation(
+                    out=h_rows[:, mh, t, cols], in_=acc[:], func=RELU, bias=bias_hid[:, mh, t : t + 1], scale=1.0
+                )
+
+        def regroup_hidden(mh, bh):
+            cols = slice(bh * B_HALF, (bh + 1) * B_HALF)
+            wide = slice(bh * B_HALF * PACK, (bh + 1) * B_HALF * PACK)
+            regroup(
+                h_grouped[:, mh, wide].rearrange("p (c t) -> p c t", t=PACK),
+                h_rows[:, mh, :, cols],
+            )
+
+        def quantise_hidden(mh, bh):
+            cols = slice(bh * B_HALF, (bh + 1) * B_HALF)
+            wide = slice(bh * B_HALF * PACK, (bh + 1) * B_HALF * PACK)
+            nc.vector.quantize_mx(
+                out=h_codes[:, mh, cols].bitcast(FP8X4), scales=h_scales[:, mh, cols], in_=h_grouped[:, mh, wide]
+            )
+
+        def regroup_w_out():
+            for g in range(PASSES):
+                regroup(
+                    wo_grouped[:, g * HALF * PACK : (g + 1) * HALF * PACK].rearrange("p (c t) -> p c t", t=PACK),
+                    wo_raw[:, g, :, :],
+                )
+
+        def quantise_w_out():
+            for c0, c1 in ((0, 512), (512, PASSES * HALF)):
+                nc.vector.quantize_mx(
+                    out=wo_codes[:, c0:c1].bitcast(FP8X4),
+                    scales=wo_scales[:, c0:c1],
+                    in_=wo_grouped[:, c0 * PACK : c1 * PACK],
+                )
+
+        def shift_pass(acc, jt, bh, g):
+            cols = slice(bh * B_HALF, (bh + 1) * B_HALF)
+            w0 = g * HALF + jt * P
+            nc.tensor.matmul_mx(
+                out=acc[:],
+                lhsT=wo_codes[:, w0 : w0 + P].bitcast(FP8X4),
+                lhsT_scale=wo_scales[:, w0 : w0 + P],
+                rhs=h_codes[:, g, cols].bitcast(FP8X4),
+                rhs_scale=h_scales[:, g, cols],
+                start=(g == 0),
+                stop=(g == PASSES - 1),
+            )
+
+        def open_shift(bh):
+            accs = [psum_acc.tile([P, B_HALF], F32, tag="acc", name="shift_acc%d" % jt) for jt in range(J_TILES)]
+            for jt in range(J_TILES):
+                shift_pass(accs[jt], jt, bh, 0)
+            return accs
+
+        def close_shift(accs, bh):
+            cols = slice(bh * B_HALF, (bh + 1) * B_HALF)
+            for jt in range(J_TILES):
+                acc = accs[jt]
+                shift_pass(acc, jt, bh, 1)
+                nc.scalar.activation(
+                    out=shift_t[:, jt, cols],
+                    in_=acc[:],
+                    func=IDENTITY,
+                    bias=bias_out[:, jt : jt + 1],
+                    scale=1.0,
+                )
+
+        def couple(bh, jt):
+            step = bh * J_TILES + jt
+            cols = slice(2 * P * jt, 2 * P * (jt + 1))
+            for pair in range(2):
+                bank = y_banks[2 * (step % 2) + pair]
+                for k in range(2):
+                    bt = 4 * bh + 2 * pair + k
+                    nc.tensor.transpose(bank[:, 2 * k + 1, :], shift_t[:, jt, bt * P : (bt + 1) * P], ident_f32[:])
+            for pair in range(2):
+                bank = y_banks[2 * (step % 2) + pair]
+                bt = 4 * bh + 2 * pair
+                y = y_pool.tile([P, 2, 2 * P], F32)
+                nc.vector.tensor_tensor(
+                    out=y[:].rearrange("p k (j e) -> p k j e", e=2),
+                    in0=bank[:].rearrange("p (k e) j -> p k j e", e=2),
+                    in1=x_rows[:, bt : bt + 2, cols].rearrange("p k (j e) -> p k j e", e=2),
+                    op=ADD,
+                )
+                nc.sync.dma_start(
+                    out=out[bt * P : (bt + 2) * P, cols].rearrange("(p k) c -> p k c", k=2), in_=y[:]
+                )
+
+        with tc.manual_schedule():
+            prepare_w_hid(0)
+            transpose_h_prev(0)
+            transpose_h_prev(1)
+            quantise_h_prev(0)
+            transpose_h_prev(2)
+            transpose_h_prev(3)
+            spread_biases()
+            quantise_h_prev(1)
+            regroup_w_out()
+            for bt in range(4, 8):
+                transpose_h_prev(bt)
+            hidden_matmuls(0, 0)
+            quantise_h_prev(2)
+            quantise_w_out()
+            quantise_h_prev(3)
+            prepare_w_hid(1)
+            hidden_matmuls(0, 1)
+            regroup_hidden(0, 0)
+            hidden_matmuls(1, 0)
+            regroup_hidden(0, 1)
+            quantise_hidden(0, 0)
+            hidden_matmuls(1, 1)
+            regroup_hidden(1, 0)
+            quantise_hidden(1, 0)
+            shift_0 = open_shift(0)
+            close_shift(shift_0, 0)
+            quantise_hidden(0, 1)
+            regroup_hidden(1, 1)
+            quantise_hidden(1, 1)
+            couple(0, 0)
+            shift_1 = open_shift(1)
+            couple(0, 1)
+            close_shift(shift_1, 1)
+            couple(0, 2)
+            for jt in range(J_TILES):
+                couple(1, jt)

@@ -22,6 +22,7 @@ B_HALF = 512
 PASSES = MP // K_PASS
 J_TILES = HALF // P
 Y_BANKS = 4
+WARM_ROUNDS = 2
 W_PIECE = 256
 
 FLOPS = 2 * B * MP * MID + 2 * B * MID * HALF
@@ -60,15 +61,15 @@ def tile_additivecoupling_pa_kernel(tc, x, h_prev, w_hid, b_hid, w_out, b_out, o
 
         ident_f32 = keep.tile([P, P], F32)
         ident_bf16 = keep.tile([P, P], BF16)
-        zeros_f32 = keep.tile([P, P], F32)
+        zeros = keep.tile([P, 4 * P], BF16)
         bias_rows = keep.tile([P, P], BF16)
         bias_hid = keep.tile([P, PASSES, PACK], BF16)
         bias_out = keep.tile([P, J_TILES], F32)
 
         y_banks = [psum_y.tile([P, 4, P], F32, name="y_bank%d" % i) for i in range(Y_BANKS)]
 
+        nc.vector.memset(zeros[:], 0.0)
         nc.vector.memset(bias_rows[:], 0.0)
-        nc.vector.memset(zeros_f32[:], 0.0)
         nc.scalar.dma_start(out=bias_rows[0:J_TILES, :], in_=b_out.rearrange("(m p) -> m p", p=P))
         nc.scalar.dma_start(out=bias_hid[:], in_=b_hid.rearrange("(g p t) -> p g t", p=P, t=PACK))
 
@@ -110,9 +111,17 @@ def tile_additivecoupling_pa_kernel(tc, x, h_prev, w_hid, b_hid, w_out, b_out, o
             bias_t = psum_acc.tile([P, P], BF16, tag="acc")
             nc.tensor.transpose(bias_t[:], bias_rows[:], ident_bf16[:])
             nc.vector.tensor_copy(out=bias_out[:], in_=bias_t[:, 0:J_TILES])
-            for bank in y_banks:
-                for k in range(2):
-                    nc.tensor.transpose(bank[:, 2 * k, :], zeros_f32[:], ident_f32[:])
+
+        def zero_y_banks():
+            for r in range(WARM_ROUNDS):
+                for bank in y_banks:
+                    nc.tensor.matmul(
+                        bank[:].rearrange("p k j -> p (k j)"),
+                        zeros[:, 0:P],
+                        zeros[:],
+                        start=(r == 0),
+                        stop=(r == WARM_ROUNDS - 1),
+                    )
 
         def transpose_h_prev(bt):
             words = hp_rows[:, bt, :].bitcast(F32)
@@ -266,6 +275,7 @@ def tile_additivecoupling_pa_kernel(tc, x, h_prev, w_hid, b_hid, w_out, b_out, o
                 )
 
         with tc.manual_schedule():
+            zero_y_banks()
             prepare_w_hid(0)
             transpose_h_prev(0)
             transpose_h_prev(1)

@@ -158,10 +158,10 @@ def tile_additivecoupling_pa_kernel(tc, x, h_prev, w_hid, b_hid, w_out, b_out, o
                 for g in range(PASSES):
                     nc.vector.tensor_copy(
                         out=w_grouped[:, mh, g, c0 * PACK : (c0 + W_PIECE) * PACK].rearrange(
-                            "p (t m j) -> p t m j", t=2, j=PACK
+                            "p (t m j) -> p m t j", t=2, j=PACK
                         ),
-                        in_=w_raw[:, mh, g, :, :].rearrange("p j (m t) -> p t m j", t=PACK)[
-                            :, 2 * piece : 2 * piece + 2, :, :
+                        in_=w_raw[:, mh, g, :, :].rearrange("p j (m t) -> p m t j", t=PACK)[
+                            :, :, 2 * piece : 2 * piece + 2, :
                         ],
                     )
                 for g in range(PASSES):

@@ -21,9 +21,9 @@ B_TILES = B // P
 B_HALF = 512
 PASSES = MP // K_PASS
 J_TILES = HALF // P
-Y_BANKS = 4
-WARM_ROUNDS = 2
-W_PIECE = 256
+ADD_BANKS = 2
+MERGE_BANKS = 2
+WARM_ROUNDS = 3
 
 FLOPS = 2 * B * MP * MID + 2 * B * MID * HALF
 
@@ -37,7 +37,9 @@ def tile_additivecoupling_pa_kernel(tc, x, h_prev, w_hid, b_hid, w_out, b_out, o
         psum_y = ctx.enter_context(tc.psum_pool(name="psum_y", bufs=1))
 
         hp_rows = keep.tile([P, B_TILES, MP], BF16)
-        hp_grouped = keep.tile([P, PASSES, B * PACK], BF16, align_bytes=64)
+        hp_grouped = [
+            keep.tile([P, PASSES, B_HALF * PACK], BF16, align_bytes=64, name="hp_grouped%d" % bh) for bh in range(2)
+        ]
         hp_codes = keep.tile([P, PASSES, B], U32, align_bytes=64)
         hp_scales = keep.tile([P, PASSES, B], U8, align_bytes=64)
 
@@ -46,7 +48,9 @@ def tile_additivecoupling_pa_kernel(tc, x, h_prev, w_hid, b_hid, w_out, b_out, o
         w_codes = keep.tile([P, PASSES, MID], U32, align_bytes=64)
         w_scales = keep.tile([P, PASSES, MID], U8, align_bytes=64)
 
-        h_rows = keep.tile([P, PASSES, PACK, B], BF16)
+        h_rows = [
+            [keep.tile([P, PACK, B_HALF], BF16, name="h_rows%d%d" % (mh, bh)) for bh in range(2)] for mh in range(2)
+        ]
         h_grouped = keep.tile([P, PASSES, B * PACK], BF16, align_bytes=64)
         h_codes = keep.tile([P, PASSES, B], U32, align_bytes=64)
         h_scales = keep.tile([P, PASSES, B], U8, align_bytes=64)
@@ -66,7 +70,8 @@ def tile_additivecoupling_pa_kernel(tc, x, h_prev, w_hid, b_hid, w_out, b_out, o
         bias_hid = keep.tile([P, PASSES, PACK], BF16)
         bias_out = keep.tile([P, J_TILES], F32)
 
-        y_banks = [psum_y.tile([P, 4, P], F32, name="y_bank%d" % i) for i in range(Y_BANKS)]
+        add_banks = [psum_y.tile([P, 4, P], F32, name="add_bank%d" % i) for i in range(ADD_BANKS)]
+        merge_banks = [psum_y.tile([P, 2, 2, P], F32, name="merge_bank%d" % i) for i in range(MERGE_BANKS)]
 
         nc.vector.memset(zeros[:], 0.0)
         nc.vector.memset(bias_rows[:], 0.0)
@@ -110,11 +115,11 @@ def tile_additivecoupling_pa_kernel(tc, x, h_prev, w_hid, b_hid, w_out, b_out, o
         def spread_biases():
             bias_t = psum_acc.tile([P, P], BF16, tag="acc")
             nc.tensor.transpose(bias_t[:], bias_rows[:], ident_bf16[:])
-            nc.vector.tensor_copy(out=bias_out[:], in_=bias_t[:, 0:J_TILES])
+            nc.scalar.copy(out=bias_out[:], in_=bias_t[:, 0:J_TILES])
 
-        def zero_y_banks():
+        def zero_add_banks():
             for r in range(WARM_ROUNDS):
-                for bank in y_banks:
+                for bank in add_banks:
                     nc.tensor.matmul(
                         bank[:].rearrange("p k j -> p (k j)"),
                         zeros[:, 0:P],
@@ -131,45 +136,44 @@ def tile_additivecoupling_pa_kernel(tc, x, h_prev, w_hid, b_hid, w_out, b_out, o
                     nc.tensor.transpose(
                         pairs_t[:, 2 * g + u, :], words[:, 2 * P * g + u : 2 * P * (g + 1) : 2], ident_f32[:]
                     )
+            b0 = (bt % 4) * P * PACK
             nc.scalar.copy(
-                out=hp_grouped[:, :, bt * P * PACK : (bt + 1) * P * PACK]
+                out=hp_grouped[bt // 4][:, :, b0 : b0 + P * PACK]
                 .bitcast(F32)
                 .rearrange("q g (b u) -> q g b u", u=2),
                 in_=pairs_t[:].rearrange("q (g u) b -> q g b u", u=2),
             )
 
-        def quantise_h_prev(pair):
-            cols = slice(pair * 2 * P, (pair + 1) * 2 * P)
-            wide = slice(pair * 2 * P * PACK, (pair + 1) * 2 * P * PACK)
+        def quantise_h_prev(bh):
+            cols = slice(bh * B_HALF, (bh + 1) * B_HALF)
             for g in range(PASSES):
                 nc.vector.quantize_mx(
-                    out=hp_codes[:, g, cols].bitcast(FP8X4), scales=hp_scales[:, g, cols], in_=hp_grouped[:, g, wide]
+                    out=hp_codes[:, g, cols].bitcast(FP8X4), scales=hp_scales[:, g, cols], in_=hp_grouped[bh][:, g, :]
                 )
 
-        def regroup(dst, src):
-            nc.vector.tensor_copy(
+        def regroup(copy, dst, src):
+            copy(
                 out=dst.rearrange("p (c i) t -> p c t i", i=4),
                 in_=src.rearrange("p t (c i) -> p c t i", i=4),
             )
 
-        def prepare_w_hid(mh):
-            for piece in range(512 // W_PIECE):
-                c0 = piece * W_PIECE
-                for g in range(PASSES):
-                    nc.vector.tensor_copy(
-                        out=w_grouped[:, mh, g, c0 * PACK : (c0 + W_PIECE) * PACK].rearrange(
-                            "p (t m j) -> p m t j", t=2, j=PACK
-                        ),
-                        in_=w_raw[:, mh, g, :, :].rearrange("p j (m t) -> p m t j", t=PACK)[
-                            :, :, 2 * piece : 2 * piece + 2, :
-                        ],
-                    )
-                for g in range(PASSES):
-                    nc.vector.quantize_mx(
-                        out=w_codes[:, g, 512 * mh + c0 : 512 * mh + c0 + W_PIECE].bitcast(FP8X4),
-                        scales=w_scales[:, g, 512 * mh + c0 : 512 * mh + c0 + W_PIECE],
-                        in_=w_grouped[:, mh, g, c0 * PACK : (c0 + W_PIECE) * PACK],
-                    )
+        def regroup_w_hid(mh, g, parts=1):
+            n = PACK // parts
+            for part in range(parts):
+                nc.vector.tensor_copy(
+                    out=w_grouped[:, mh, g, :].rearrange("p (t m j) -> p m t j", t=PACK, j=PACK)[
+                        :, :, n * part : n * (part + 1), :
+                    ],
+                    in_=w_raw[:, mh, g, :, :].rearrange("p j (m t) -> p m t j", t=PACK)[
+                        :, :, n * part : n * (part + 1), :
+                    ],
+                )
+
+        def quantise_w_hid(mh, g):
+            cols = slice(512 * mh, 512 * (mh + 1))
+            nc.vector.quantize_mx(
+                out=w_codes[:, g, cols].bitcast(FP8X4), scales=w_scales[:, g, cols], in_=w_grouped[:, mh, g, :]
+            )
 
         def hidden_matmuls(mh, bh):
             cols = slice(bh * B_HALF, (bh + 1) * B_HALF)
@@ -187,15 +191,15 @@ def tile_additivecoupling_pa_kernel(tc, x, h_prev, w_hid, b_hid, w_out, b_out, o
                         stop=(g == PASSES - 1),
                     )
                 nc.scalar.activation(
-                    out=h_rows[:, mh, t, cols], in_=acc[:], func=RELU, bias=bias_hid[:, mh, t : t + 1], scale=1.0
+                    out=h_rows[mh][bh][:, t, :], in_=acc[:], func=RELU, bias=bias_hid[:, mh, t : t + 1], scale=1.0
                 )
 
         def regroup_hidden(mh, bh):
-            cols = slice(bh * B_HALF, (bh + 1) * B_HALF)
             wide = slice(bh * B_HALF * PACK, (bh + 1) * B_HALF * PACK)
             regroup(
+                nc.vector.tensor_copy,
                 h_grouped[:, mh, wide].rearrange("p (c t) -> p c t", t=PACK),
-                h_rows[:, mh, :, cols],
+                h_rows[mh][bh][:],
             )
 
         def quantise_hidden(mh, bh):
@@ -205,12 +209,12 @@ def tile_additivecoupling_pa_kernel(tc, x, h_prev, w_hid, b_hid, w_out, b_out, o
                 out=h_codes[:, mh, cols].bitcast(FP8X4), scales=h_scales[:, mh, cols], in_=h_grouped[:, mh, wide]
             )
 
-        def regroup_w_out():
-            for g in range(PASSES):
-                regroup(
-                    wo_grouped[:, g * HALF * PACK : (g + 1) * HALF * PACK].rearrange("p (c t) -> p c t", t=PACK),
-                    wo_raw[:, g, :, :],
-                )
+        def regroup_w_out(copy, g):
+            regroup(
+                copy,
+                wo_grouped[:, g * HALF * PACK : (g + 1) * HALF * PACK].rearrange("p (c t) -> p c t", t=PACK),
+                wo_raw[:, g, :, :],
+            )
 
         def quantise_w_out():
             for c0, c1 in ((0, 512), (512, PASSES * HALF)):
@@ -252,63 +256,111 @@ def tile_additivecoupling_pa_kernel(tc, x, h_prev, w_hid, b_hid, w_out, b_out, o
                     scale=1.0,
                 )
 
-        def couple(bh, jt):
-            step = bh * J_TILES + jt
-            cols = slice(2 * P * jt, 2 * P * (jt + 1))
-            for pair in range(2):
-                bank = y_banks[2 * (step % 2) + pair]
-                for k in range(2):
-                    bt = 4 * bh + 2 * pair + k
-                    nc.tensor.transpose(bank[:, 2 * k + 1, :], shift_t[:, jt, bt * P : (bt + 1) * P], ident_f32[:])
-            for pair in range(2):
-                bank = y_banks[2 * (step % 2) + pair]
-                bt = 4 * bh + 2 * pair
-                y = y_pool.tile([P, 2, 2 * P], F32)
-                nc.vector.tensor_tensor(
-                    out=y[:].rearrange("p k (j e) -> p k j e", e=2),
-                    in0=bank[:].rearrange("p (k e) j -> p k j e", e=2),
-                    in1=x_rows[:, bt : bt + 2, cols].rearrange("p k (j e) -> p k j e", e=2),
-                    op=ADD,
-                )
-                nc.sync.dma_start(
-                    out=out[bt * P : (bt + 2) * P, cols].rearrange("(p k) c -> p k c", k=2), in_=y[:]
+        def y_columns(jt):
+            return slice(2 * P * jt, 2 * P * (jt + 1))
+
+        def store_y(bt, jt, y):
+            nc.sync.dma_start(
+                out=out[bt * P : (bt + 2) * P, y_columns(jt)].rearrange("(p k) c -> p k c", k=2), in_=y[:]
+            )
+
+        def turn_back(bank, bt, jt):
+            for k in range(2):
+                nc.tensor.transpose(
+                    bank[:, 2 * k + 1, :], shift_t[:, jt, (bt + k) * P : (bt + k + 1) * P], ident_f32[:]
                 )
 
+        def add_on_vector(bank, bt, jt):
+            y = y_pool.tile([P, 2, 2 * P], F32)
+            nc.vector.tensor_tensor(
+                out=y[:].rearrange("p k (j e) -> p k j e", e=2),
+                in0=bank[:].rearrange("p (k e) j -> p k j e", e=2),
+                in1=x_rows[:, bt : bt + 2, y_columns(jt)].rearrange("p k (j e) -> p k j e", e=2),
+                op=ADD,
+            )
+            store_y(bt, jt, y)
+
+        def merge_x(bank, bt, jt):
+            nc.tensor.matmul(
+                bank[:],
+                ident_bf16[:],
+                x_rows[:, bt : bt + 2, y_columns(jt)].rearrange("p k (j e) -> p k e j", e=2),
+                start=True,
+                stop=False,
+            )
+
+        def merge_shift(bank, bt, jt):
+            for k in range(2):
+                nc.tensor.matmul(
+                    bank[:, k, 1, :],
+                    shift_t[:, jt, (bt + k) * P : (bt + k + 1) * P],
+                    ident_f32[:],
+                    start=False,
+                    stop=(k == 1),
+                )
+
+        def copy_on_scalar(bank, bt, jt):
+            y = y_pool.tile([P, 2, 2 * P], F32)
+            nc.scalar.copy(
+                out=y[:].rearrange("p k (j e) -> p k j e", e=2), in_=bank[:].rearrange("p k e j -> p k j e")
+            )
+            store_y(bt, jt, y)
+
         with tc.manual_schedule():
-            zero_y_banks()
-            prepare_w_hid(0)
-            transpose_h_prev(0)
-            transpose_h_prev(1)
+            vector, scalar = nc.vector.tensor_copy, nc.scalar.copy
+            zero_add_banks()
+            for g in range(PASSES):
+                regroup_w_hid(0, g, parts=2)
+            for g in range(PASSES):
+                quantise_w_hid(0, g)
+            for bt in range(4):
+                transpose_h_prev(bt)
+            regroup_w_out(vector, 0)
+            regroup_w_out(scalar, 1)
             quantise_h_prev(0)
-            transpose_h_prev(2)
-            transpose_h_prev(3)
-            spread_biases()
-            quantise_h_prev(1)
-            regroup_w_out()
             for bt in range(4, 8):
                 transpose_h_prev(bt)
             hidden_matmuls(0, 0)
-            quantise_h_prev(2)
+            spread_biases()
             quantise_w_out()
-            quantise_h_prev(3)
-            prepare_w_hid(1)
+            regroup_w_hid(1, 0)
+            quantise_h_prev(1)
             hidden_matmuls(0, 1)
+            regroup_w_hid(1, 1)
+            for g in range(PASSES):
+                quantise_w_hid(1, g)
             regroup_hidden(0, 0)
             hidden_matmuls(1, 0)
             regroup_hidden(0, 1)
             quantise_hidden(0, 0)
             hidden_matmuls(1, 1)
             regroup_hidden(1, 0)
+            quantise_hidden(0, 1)
             quantise_hidden(1, 0)
             shift_0 = open_shift(0)
             close_shift(shift_0, 0)
-            quantise_hidden(0, 1)
             regroup_hidden(1, 1)
+            for pair in range(2):
+                turn_back(add_banks[pair], 2 * pair, 0)
+            for pair in range(2):
+                add_on_vector(add_banks[pair], 2 * pair, 0)
             quantise_hidden(1, 1)
-            couple(0, 0)
             shift_1 = open_shift(1)
-            couple(0, 1)
+            for jt in range(2):
+                merge_x(merge_banks[jt], 6, jt)
+            for pair in range(2):
+                turn_back(add_banks[pair], 2 * pair, 1)
+            for pair in range(2):
+                add_on_vector(add_banks[pair], 2 * pair, 1)
             close_shift(shift_1, 1)
-            couple(0, 2)
+            for pair in range(2):
+                turn_back(add_banks[pair], 2 * pair, 2)
+            for pair in range(2):
+                add_on_vector(add_banks[pair], 2 * pair, 2)
             for jt in range(J_TILES):
-                couple(1, jt)
+                if jt == 2:
+                    merge_x(merge_banks[0], 6, jt)
+                merge_shift(merge_banks[jt % 2], 6, jt)
+                turn_back(add_banks[jt % 2], 4, jt)
+                add_on_vector(add_banks[jt % 2], 4, jt)
+                copy_on_scalar(merge_banks[jt % 2], 6, jt)

@@ -32,7 +32,6 @@ def tile_additivecoupling_pa_kernel(tc, x, h_prev, w_hid, b_hid, w_out, b_out, o
     nc = tc.nc
     with ExitStack() as ctx:
         keep = ctx.enter_context(tc.tile_pool(name="keep", bufs=1))
-        y_pool = ctx.enter_context(tc.tile_pool(name="y_pool", bufs=12))
         psum_acc = ctx.enter_context(tc.psum_pool(name="psum_acc", bufs=4))
         psum_y = ctx.enter_context(tc.psum_pool(name="psum_y", bufs=1))
 
@@ -61,22 +60,24 @@ def tile_additivecoupling_pa_kernel(tc, x, h_prev, w_hid, b_hid, w_out, b_out, o
         wo_scales = keep.tile([P, PASSES * HALF], U8, align_bytes=64)
 
         x_rows = keep.tile([P, B_TILES, D], BF16)
+        y_rows = [keep.tile([P, 2, D], F32, name="y_rows%d" % i) for i in range(B_TILES // 2)]
         shift_t = keep.tile([P, J_TILES, B], F32)
 
         ident_f32 = keep.tile([P, P], F32)
         ident_bf16 = keep.tile([P, P], BF16)
         zeros = keep.tile([P, 4 * P], BF16)
-        bias_rows = keep.tile([P, P], BF16)
-        bias_hid = keep.tile([P, PASSES, PACK], BF16)
-        bias_out = keep.tile([P, J_TILES], F32)
+        bias_rows = keep.tile([P, PACK * P], BF16)
+        bias_cols = keep.tile([P, PACK + 1, PASSES + J_TILES], F32)
 
         add_banks = [psum_y.tile([P, 4, P], F32, name="add_bank%d" % i) for i in range(ADD_BANKS)]
         merge_banks = [psum_y.tile([P, 2, 2, P], F32, name="merge_bank%d" % i) for i in range(MERGE_BANKS)]
 
         nc.vector.memset(zeros[:], 0.0)
         nc.vector.memset(bias_rows[:], 0.0)
-        nc.scalar.dma_start(out=bias_rows[0:J_TILES, :], in_=b_out.rearrange("(m p) -> m p", p=P))
-        nc.scalar.dma_start(out=bias_hid[:], in_=b_hid.rearrange("(g p t) -> p g t", p=P, t=PACK))
+        nc.scalar.dma_start(out=bias_rows[0:PASSES, :], in_=b_hid.rearrange("(m c) -> m c", m=PASSES))
+        nc.scalar.dma_start(
+            out=bias_rows[PASSES : PASSES + J_TILES, 0:P], in_=b_out.rearrange("(m p) -> m p", p=P)
+        )
 
         def load_h_prev(duo):
             nc.sync.dma_start(
@@ -113,9 +114,11 @@ def tile_additivecoupling_pa_kernel(tc, x, h_prev, w_hid, b_hid, w_out, b_out, o
         nc.vector.tensor_copy(out=ident_bf16[:], in_=ident_f32[:])
 
         def spread_biases():
-            bias_t = psum_acc.tile([P, P], BF16, tag="acc")
-            nc.tensor.transpose(bias_t[:], bias_rows[:], ident_bf16[:])
-            nc.scalar.copy(out=bias_out[:], in_=bias_t[:, 0:J_TILES])
+            bias_t = psum_acc.tile([P, PACK + 1, P], BF16, tag="acc")
+            for t in range(PACK):
+                nc.tensor.transpose(bias_t[:, t, :], bias_rows[:, t : PACK * P : PACK], ident_bf16[:])
+            nc.tensor.transpose(bias_t[:, PACK, :], bias_rows[:, 0:P], ident_bf16[:])
+            nc.scalar.copy(out=bias_cols[:], in_=bias_t[:, :, 0 : PASSES + J_TILES])
 
         def zero_add_banks():
             for r in range(WARM_ROUNDS):
@@ -191,7 +194,7 @@ def tile_additivecoupling_pa_kernel(tc, x, h_prev, w_hid, b_hid, w_out, b_out, o
                         stop=(g == PASSES - 1),
                     )
                 nc.scalar.activation(
-                    out=h_rows[mh][bh][:, t, :], in_=acc[:], func=RELU, bias=bias_hid[:, mh, t : t + 1], scale=1.0
+                    out=h_rows[mh][bh][:, t, :], in_=acc[:], func=RELU, bias=bias_cols[:, t, mh : mh + 1], scale=1.0
                 )
 
         def regroup_hidden(mh, bh):
@@ -252,17 +255,24 @@ def tile_additivecoupling_pa_kernel(tc, x, h_prev, w_hid, b_hid, w_out, b_out, o
                     out=shift_t[:, jt, cols],
                     in_=acc[:],
                     func=IDENTITY,
-                    bias=bias_out[:, jt : jt + 1],
+                    bias=bias_cols[:, PACK, PASSES + jt : PASSES + jt + 1],
                     scale=1.0,
                 )
 
         def y_columns(jt):
             return slice(2 * P * jt, 2 * P * (jt + 1))
 
-        def store_y(bt, jt, y):
+        def store_y(bt, cols):
             nc.sync.dma_start(
-                out=out[bt * P : (bt + 2) * P, y_columns(jt)].rearrange("(p k) c -> p k c", k=2), in_=y[:]
+                out=out[bt * P : (bt + 2) * P, cols].rearrange("(p k) c -> p k c", k=2),
+                in_=y_rows[bt // 2][:, :, cols],
             )
+
+        def unit_done(bt, jt):
+            if jt == 1:
+                store_y(bt, slice(0, 4 * P))
+            elif jt == 2:
+                store_y(bt, y_columns(2))
 
         def turn_back(bank, bt, jt):
             for k in range(2):
@@ -271,14 +281,13 @@ def tile_additivecoupling_pa_kernel(tc, x, h_prev, w_hid, b_hid, w_out, b_out, o
                 )
 
         def add_on_vector(bank, bt, jt):
-            y = y_pool.tile([P, 2, 2 * P], F32)
             nc.vector.tensor_tensor(
-                out=y[:].rearrange("p k (j e) -> p k j e", e=2),
+                out=y_rows[bt // 2][:, :, y_columns(jt)].rearrange("p k (j e) -> p k j e", e=2),
                 in0=bank[:].rearrange("p (k e) j -> p k j e", e=2),
                 in1=x_rows[:, bt : bt + 2, y_columns(jt)].rearrange("p k (j e) -> p k j e", e=2),
                 op=ADD,
             )
-            store_y(bt, jt, y)
+            unit_done(bt, jt)
 
         def merge_x(bank, bt, jt):
             nc.tensor.matmul(
@@ -300,11 +309,10 @@ def tile_additivecoupling_pa_kernel(tc, x, h_prev, w_hid, b_hid, w_out, b_out, o
                 )
 
         def copy_on_scalar(bank, bt, jt):
-            y = y_pool.tile([P, 2, 2 * P], F32)
             nc.scalar.copy(
-                out=y[:].rearrange("p k (j e) -> p k j e", e=2), in_=bank[:].rearrange("p k e j -> p k j e")
+                out=y_rows[bt // 2][:, :, y_columns(jt)].rearrange("p k (j e) -> p k j e", e=2), in_=bank[:].rearrange("p k e j -> p k j e")
             )
-            store_y(bt, jt, y)
+            unit_done(bt, jt)
 
         with tc.manual_schedule():
             vector, scalar = nc.vector.tensor_copy, nc.scalar.copy
@@ -320,8 +328,8 @@ def tile_additivecoupling_pa_kernel(tc, x, h_prev, w_hid, b_hid, w_out, b_out, o
             quantise_h_prev(0)
             for bt in range(4, 8):
                 transpose_h_prev(bt)
-            hidden_matmuls(0, 0)
             spread_biases()
+            hidden_matmuls(0, 0)
             quantise_w_out()
             regroup_w_hid(1, 0)
             quantise_h_prev(1)

@@ -60,7 +60,8 @@ def tile_additivecoupling_pa_kernel(tc, x, h_prev, w_hid, b_hid, w_out, b_out, o
         wo_scales = keep.tile([P, PASSES * HALF], U8, align_bytes=64)
 
         x_rows = keep.tile([P, B_TILES, D], BF16)
-        y_rows = [keep.tile([P, 2, D], F32, name="y_rows%d" % i) for i in range(B_TILES // 2)]
+        y_wide = [keep.tile([P, 2, 4 * P], F32, name="y_wide%d" % i) for i in range(B_TILES // 2)]
+        y_last = [keep.tile([P, 2, 2 * P], F32, name="y_last%d" % i) for i in range(B_TILES // 2)]
         shift_t = keep.tile([P, J_TILES, B], F32)
 
         ident_f32 = keep.tile([P, P], F32)
@@ -163,13 +164,12 @@ def tile_additivecoupling_pa_kernel(tc, x, h_prev, w_hid, b_hid, w_out, b_out, o
         def regroup_w_hid(mh, g, parts=1):
             n = PACK // parts
             for part in range(parts):
+                for_t = slice(n * part, n * (part + 1))
                 nc.vector.tensor_copy(
-                    out=w_grouped[:, mh, g, :].rearrange("p (t m j) -> p m t j", t=PACK, j=PACK)[
-                        :, :, n * part : n * (part + 1), :
+                    out=w_grouped[:, mh, g, :].rearrange("p (t m i j) -> p m t j i", t=PACK, i=2, j=PACK)[
+                        :, :, for_t, :, :
                     ],
-                    in_=w_raw[:, mh, g, :, :].rearrange("p j (m t) -> p m t j", t=PACK)[
-                        :, :, n * part : n * (part + 1), :
-                    ],
+                    in_=w_raw[:, mh, g, :, :].rearrange("p j (m i t) -> p m t j i", t=PACK, i=2)[:, :, for_t, :, :],
                 )
 
         def quantise_w_hid(mh, g):
@@ -262,17 +262,16 @@ def tile_additivecoupling_pa_kernel(tc, x, h_prev, w_hid, b_hid, w_out, b_out, o
         def y_columns(jt):
             return slice(2 * P * jt, 2 * P * (jt + 1))
 
-        def store_y(bt, cols):
-            nc.sync.dma_start(
-                out=out[bt * P : (bt + 2) * P, cols].rearrange("(p k) c -> p k c", k=2),
-                in_=y_rows[bt // 2][:, :, cols],
-            )
+        def y_unit(bt, jt):
+            tile = y_last[bt // 2][:] if jt == 2 else y_wide[bt // 2][:, :, y_columns(jt)]
+            return tile.rearrange("p k (j e) -> p k j e", e=2)
 
         def unit_done(bt, jt):
-            if jt == 1:
-                store_y(bt, slice(0, 4 * P))
-            elif jt == 2:
-                store_y(bt, y_columns(2))
+            if jt > 0:
+                cols, tile = (slice(0, 4 * P), y_wide[bt // 2]) if jt == 1 else (y_columns(2), y_last[bt // 2])
+                nc.sync.dma_start(
+                    out=out[bt * P : (bt + 2) * P, cols].rearrange("(p k) c -> p k c", k=2), in_=tile[:]
+                )
 
         def turn_back(bank, bt, jt):
             for k in range(2):
@@ -282,7 +281,7 @@ def tile_additivecoupling_pa_kernel(tc, x, h_prev, w_hid, b_hid, w_out, b_out, o
 
         def add_on_vector(bank, bt, jt):
             nc.vector.tensor_tensor(
-                out=y_rows[bt // 2][:, :, y_columns(jt)].rearrange("p k (j e) -> p k j e", e=2),
+                out=y_unit(bt, jt),
                 in0=bank[:].rearrange("p (k e) j -> p k j e", e=2),
                 in1=x_rows[:, bt : bt + 2, y_columns(jt)].rearrange("p k (j e) -> p k j e", e=2),
                 op=ADD,
@@ -310,7 +309,7 @@ def tile_additivecoupling_pa_kernel(tc, x, h_prev, w_hid, b_hid, w_out, b_out, o
 
         def copy_on_scalar(bank, bt, jt):
             nc.scalar.copy(
-                out=y_rows[bt // 2][:, :, y_columns(jt)].rearrange("p k (j e) -> p k j e", e=2), in_=bank[:].rearrange("p k e j -> p k j e")
+                out=y_unit(bt, jt), in_=bank[:].rearrange("p k e j -> p k j e")
             )
             unit_done(bt, jt)
 

@@ -32,6 +32,7 @@ def tile_additivecoupling_pa_kernel(tc, x, h_prev, w_hid, b_hid, w_out, b_out, o
     nc = tc.nc
     with ExitStack() as ctx:
         keep = ctx.enter_context(tc.tile_pool(name="keep", bufs=1))
+        y_pool = ctx.enter_context(tc.tile_pool(name="y_pool", bufs=12))
         psum_acc = ctx.enter_context(tc.psum_pool(name="psum_acc", bufs=4))
         psum_y = ctx.enter_context(tc.psum_pool(name="psum_y", bufs=1))
 
@@ -60,8 +61,6 @@ def tile_additivecoupling_pa_kernel(tc, x, h_prev, w_hid, b_hid, w_out, b_out, o
         wo_scales = keep.tile([P, PASSES * HALF], U8, align_bytes=64)
 
         x_rows = keep.tile([P, B_TILES, D], BF16)
-        y_wide = [keep.tile([P, 2, 4 * P], F32, name="y_wide%d" % i) for i in range(B_TILES // 2)]
-        y_last = [keep.tile([P, 2, 2 * P], F32, name="y_last%d" % i) for i in range(B_TILES // 2)]
         shift_t = keep.tile([P, J_TILES, B], F32)
 
         ident_f32 = keep.tile([P, P], F32)
@@ -96,15 +95,13 @@ def tile_additivecoupling_pa_kernel(tc, x, h_prev, w_hid, b_hid, w_out, b_out, o
                 )
 
         load_w_hid(0)
-        for duo in range(2):
+        for duo in range(4):
             load_h_prev(duo)
+        load_w_hid(1)
         nc.sync.dma_start(
             out=wo_raw[:].rearrange("p g t n -> p g (t n)"),
             in_=w_out.rearrange("(g p t) n -> p g (t n)", p=P, t=PACK),
         )
-        for duo in range(2, 4):
-            load_h_prev(duo)
-        load_w_hid(1)
         for xh in range(2):
             nc.sync.dma_start(
                 out=x_rows[:, 4 * xh : 4 * xh + 4, :].rearrange("p (c k) d -> p c (k d)", k=2),
@@ -132,7 +129,7 @@ def tile_additivecoupling_pa_kernel(tc, x, h_prev, w_hid, b_hid, w_out, b_out, o
                         stop=(r == WARM_ROUNDS - 1),
                     )
 
-        def transpose_h_prev(bt):
+        def transpose_h_prev(bt, copy=nc.scalar.copy):
             words = hp_rows[:, bt, :].bitcast(F32)
             pairs_t = psum_acc.tile([P, 2 * PASSES, P], F32, tag="acc")
             for g in range(PASSES):
@@ -141,7 +138,7 @@ def tile_additivecoupling_pa_kernel(tc, x, h_prev, w_hid, b_hid, w_out, b_out, o
                         pairs_t[:, 2 * g + u, :], words[:, 2 * P * g + u : 2 * P * (g + 1) : 2], ident_f32[:]
                     )
             b0 = (bt % 4) * P * PACK
-            nc.scalar.copy(
+            copy(
                 out=hp_grouped[bt // 4][:, :, b0 : b0 + P * PACK]
                 .bitcast(F32)
                 .rearrange("q g (b u) -> q g b u", u=2),
@@ -240,38 +237,29 @@ def tile_additivecoupling_pa_kernel(tc, x, h_prev, w_hid, b_hid, w_out, b_out, o
                 stop=(g == PASSES - 1),
             )
 
-        def open_shift(bh):
-            accs = [psum_acc.tile([P, B_HALF], F32, tag="acc", name="shift_acc%d" % jt) for jt in range(J_TILES)]
-            for jt in range(J_TILES):
-                shift_pass(accs[jt], jt, bh, 0)
-            return accs
+        def open_shift(jt, bh):
+            acc = psum_acc.tile([P, B_HALF], F32, tag="acc", name="shift_acc%d" % jt)
+            shift_pass(acc, jt, bh, 0)
+            return acc
 
-        def close_shift(accs, bh):
+        def close_shift(acc, jt, bh):
             cols = slice(bh * B_HALF, (bh + 1) * B_HALF)
-            for jt in range(J_TILES):
-                acc = accs[jt]
-                shift_pass(acc, jt, bh, 1)
-                nc.scalar.activation(
-                    out=shift_t[:, jt, cols],
-                    in_=acc[:],
-                    func=IDENTITY,
-                    bias=bias_cols[:, PACK, PASSES + jt : PASSES + jt + 1],
-                    scale=1.0,
-                )
+            shift_pass(acc, jt, bh, 1)
+            nc.scalar.activation(
+                out=shift_t[:, jt, cols],
+                in_=acc[:],
+                func=IDENTITY,
+                bias=bias_cols[:, PACK, PASSES + jt : PASSES + jt + 1],
+                scale=1.0,
+            )
 
         def y_columns(jt):
             return slice(2 * P * jt, 2 * P * (jt + 1))
 
-        def y_unit(bt, jt):
-            tile = y_last[bt // 2][:] if jt == 2 else y_wide[bt // 2][:, :, y_columns(jt)]
-            return tile.rearrange("p k (j e) -> p k j e", e=2)
-
-        def unit_done(bt, jt):
-            if jt > 0:
-                cols, tile = (slice(0, 4 * P), y_wide[bt // 2]) if jt == 1 else (y_columns(2), y_last[bt // 2])
-                nc.sync.dma_start(
-                    out=out[bt * P : (bt + 2) * P, cols].rearrange("(p k) c -> p k c", k=2), in_=tile[:]
-                )
+        def store_y(bt, jt, y):
+            nc.sync.dma_start(
+                out=out[bt * P : (bt + 2) * P, y_columns(jt)].rearrange("(p k) c -> p k c", k=2), in_=y[:]
+            )
 
         def turn_back(bank, bt, jt):
             for k in range(2):
@@ -280,13 +268,14 @@ def tile_additivecoupling_pa_kernel(tc, x, h_prev, w_hid, b_hid, w_out, b_out, o
                 )
 
         def add_on_vector(bank, bt, jt):
+            y = y_pool.tile([P, 2, 2 * P], F32)
             nc.vector.tensor_tensor(
-                out=y_unit(bt, jt),
+                out=y[:].rearrange("p k (j e) -> p k j e", e=2),
                 in0=bank[:].rearrange("p (k e) j -> p k j e", e=2),
                 in1=x_rows[:, bt : bt + 2, y_columns(jt)].rearrange("p k (j e) -> p k j e", e=2),
                 op=ADD,
             )
-            unit_done(bt, jt)
+            store_y(bt, jt, y)
 
         def merge_x(bank, bt, jt):
             nc.tensor.matmul(
@@ -308,10 +297,11 @@ def tile_additivecoupling_pa_kernel(tc, x, h_prev, w_hid, b_hid, w_out, b_out, o
                 )
 
         def copy_on_scalar(bank, bt, jt):
+            y = y_pool.tile([P, 2, 2 * P], F32)
             nc.scalar.copy(
-                out=y_unit(bt, jt), in_=bank[:].rearrange("p k e j -> p k j e")
+                out=y[:].rearrange("p k (j e) -> p k j e", e=2), in_=bank[:].rearrange("p k e j -> p k j e")
             )
-            unit_done(bt, jt)
+            store_y(bt, jt, y)
 
         with tc.manual_schedule():
             vector, scalar = nc.vector.tensor_copy, nc.scalar.copy
@@ -321,15 +311,13 @@ def tile_additivecoupling_pa_kernel(tc, x, h_prev, w_hid, b_hid, w_out, b_out, o
             for g in range(PASSES):
                 quantise_w_hid(0, g)
             for bt in range(4):
-                transpose_h_prev(bt)
-            regroup_w_out(vector, 0)
-            regroup_w_out(scalar, 1)
+                transpose_h_prev(bt, vector if bt % 2 else scalar)
             quantise_h_prev(0)
             for bt in range(4, 8):
                 transpose_h_prev(bt)
             spread_biases()
             hidden_matmuls(0, 0)
-            quantise_w_out()
+            regroup_w_out(scalar, 1)
             regroup_w_hid(1, 0)
             quantise_h_prev(1)
             hidden_matmuls(0, 1)
@@ -338,36 +326,47 @@ def tile_additivecoupling_pa_kernel(tc, x, h_prev, w_hid, b_hid, w_out, b_out, o
                 quantise_w_hid(1, g)
             regroup_hidden(0, 0)
             hidden_matmuls(1, 0)
-            regroup_hidden(0, 1)
+            regroup_w_out(vector, 0)
             quantise_hidden(0, 0)
+            regroup_hidden(0, 1)
             hidden_matmuls(1, 1)
+            quantise_w_out()
             regroup_hidden(1, 0)
             quantise_hidden(0, 1)
             quantise_hidden(1, 0)
-            shift_0 = open_shift(0)
-            close_shift(shift_0, 0)
-            regroup_hidden(1, 1)
-            for pair in range(2):
-                turn_back(add_banks[pair], 2 * pair, 0)
-            for pair in range(2):
-                add_on_vector(add_banks[pair], 2 * pair, 0)
-            quantise_hidden(1, 1)
-            shift_1 = open_shift(1)
             for jt in range(2):
-                merge_x(merge_banks[jt], 6, jt)
-            for pair in range(2):
-                turn_back(add_banks[pair], 2 * pair, 1)
-            for pair in range(2):
-                add_on_vector(add_banks[pair], 2 * pair, 1)
-            close_shift(shift_1, 1)
-            for pair in range(2):
-                turn_back(add_banks[pair], 2 * pair, 2)
-            for pair in range(2):
-                add_on_vector(add_banks[pair], 2 * pair, 2)
+                merge_x(merge_banks[jt], 2, jt)
+            shift_0 = [open_shift(jt, 0) for jt in range(J_TILES)]
             for jt in range(J_TILES):
-                if jt == 2:
-                    merge_x(merge_banks[0], 6, jt)
-                merge_shift(merge_banks[jt % 2], 6, jt)
-                turn_back(add_banks[jt % 2], 4, jt)
-                add_on_vector(add_banks[jt % 2], 4, jt)
-                copy_on_scalar(merge_banks[jt % 2], 6, jt)
+                close_shift(shift_0[jt], jt, 0)
+            regroup_hidden(1, 1)
+            quantise_hidden(1, 1)
+            turn_back(add_banks[0], 0, 0)
+            add_on_vector(add_banks[0], 0, 0)
+            merge_shift(merge_banks[0], 2, 0)
+            copy_on_scalar(merge_banks[0], 2, 0)
+            turn_back(add_banks[1], 0, 1)
+            add_on_vector(add_banks[1], 0, 1)
+            close_shift(open_shift(0, 1), 0, 1)
+            turn_back(add_banks[0], 0, 2)
+            add_on_vector(add_banks[0], 0, 2)
+            close_shift(open_shift(1, 1), 1, 1)
+            turn_back(add_banks[1], 2, 2)
+            add_on_vector(add_banks[1], 2, 2)
+            close_shift(open_shift(2, 1), 2, 1)
+            merge_x(merge_banks[0], 6, 0)
+            turn_back(add_banks[0], 4, 0)
+            add_on_vector(add_banks[0], 4, 0)
+            merge_shift(merge_banks[1], 2, 1)
+            copy_on_scalar(merge_banks[1], 2, 1)
+            turn_back(add_banks[1], 4, 1)
+            add_on_vector(add_banks[1], 4, 1)
+            turn_back(add_banks[0], 4, 2)
+            add_on_vector(add_banks[0], 4, 2)
+            merge_shift(merge_banks[0], 6, 0)
+            copy_on_scalar(merge_banks[0], 6, 0)
+            turn_back(add_banks[1], 6, 2)
+            add_on_vector(add_banks[1], 6, 2)
+            merge_x(merge_banks[1], 6, 1)
+            merge_shift(merge_banks[1], 6, 1)
+            copy_on_scalar(merge_banks[1], 6, 1)

@@ -216,13 +216,12 @@ def tile_additivecoupling_pa_kernel(tc, x, h_prev, w_hid, b_hid, w_out, b_out, o
                 wo_raw[:, g, :, :],
             )
 
-        def quantise_w_out():
-            for c0, c1 in ((0, 512), (512, PASSES * HALF)):
-                nc.vector.quantize_mx(
-                    out=wo_codes[:, c0:c1].bitcast(FP8X4),
-                    scales=wo_scales[:, c0:c1],
-                    in_=wo_grouped[:, c0 * PACK : c1 * PACK],
-                )
+        def quantise_w_out(c0, c1):
+            nc.vector.quantize_mx(
+                out=wo_codes[:, c0:c1].bitcast(FP8X4),
+                scales=wo_scales[:, c0:c1],
+                in_=wo_grouped[:, c0 * PACK : c1 * PACK],
+            )
 
         def shift_pass(acc, jt, bh, g):
             cols = slice(bh * B_HALF, (bh + 1) * B_HALF)
@@ -330,23 +329,26 @@ def tile_additivecoupling_pa_kernel(tc, x, h_prev, w_hid, b_hid, w_out, b_out, o
             quantise_hidden(0, 0)
             regroup_hidden(0, 1)
             hidden_matmuls(1, 1)
-            quantise_w_out()
+            quantise_w_out(0, 512)
             regroup_hidden(1, 0)
-            quantise_hidden(0, 1)
+            quantise_w_out(512, PASSES * HALF)
             quantise_hidden(1, 0)
+            quantise_hidden(0, 1)
             for jt in range(2):
                 merge_x(merge_banks[jt], 2, jt)
             shift_0 = [open_shift(jt, 0) for jt in range(J_TILES)]
             for jt in range(J_TILES):
                 close_shift(shift_0[jt], jt, 0)
             regroup_hidden(1, 1)
-            quantise_hidden(1, 1)
             turn_back(add_banks[0], 0, 0)
             add_on_vector(add_banks[0], 0, 0)
             merge_shift(merge_banks[0], 2, 0)
             copy_on_scalar(merge_banks[0], 2, 0)
+            quantise_hidden(1, 1)
             turn_back(add_banks[1], 0, 1)
             add_on_vector(add_banks[1], 0, 1)
+            merge_shift(merge_banks[1], 2, 1)
+            copy_on_scalar(merge_banks[1], 2, 1)
             close_shift(open_shift(0, 1), 0, 1)
             turn_back(add_banks[0], 0, 2)
             add_on_vector(add_banks[0], 0, 2)
@@ -357,16 +359,14 @@ def tile_additivecoupling_pa_kernel(tc, x, h_prev, w_hid, b_hid, w_out, b_out, o
             merge_x(merge_banks[0], 6, 0)
             turn_back(add_banks[0], 4, 0)
             add_on_vector(add_banks[0], 4, 0)
-            merge_shift(merge_banks[1], 2, 1)
-            copy_on_scalar(merge_banks[1], 2, 1)
-            turn_back(add_banks[1], 4, 1)
-            add_on_vector(add_banks[1], 4, 1)
-            turn_back(add_banks[0], 4, 2)
-            add_on_vector(add_banks[0], 4, 2)
             merge_shift(merge_banks[0], 6, 0)
             copy_on_scalar(merge_banks[0], 6, 0)
-            turn_back(add_banks[1], 6, 2)
-            add_on_vector(add_banks[1], 6, 2)
+            turn_back(add_banks[1], 4, 1)
+            add_on_vector(add_banks[1], 4, 1)
             merge_x(merge_banks[1], 6, 1)
+            turn_back(add_banks[0], 4, 2)
+            add_on_vector(add_banks[0], 4, 2)
             merge_shift(merge_banks[1], 6, 1)
             copy_on_scalar(merge_banks[1], 6, 1)
+            turn_back(add_banks[1], 6, 2)
+            add_on_vector(add_banks[1], 6, 2)

from contextlib import ExitStack

import concourse.mybir as mybir
from concourse.masks import make_identity

F32 = mybir.dt.float32
BF16 = mybir.dt.bfloat16
U32 = mybir.dt.uint32
U8 = mybir.dt.uint8
FP8X4 = mybir.dt.float8_e4m3fn_x4
ADD = mybir.AluOpType.add
RELU = mybir.ActivationFunctionType.Relu
IDENTITY = mybir.ActivationFunctionType.Identity

P = 128
PACK = 4
K_PASS = P * PACK
B, D, MP, MID = 1024, 768, 1024, 1024
HALF = D // 2
B_TILES = B // P
B_HALF = 512
PASSES = MP // K_PASS
J_TILES = HALF // P
ADD_BANKS = 2
MERGE_BANKS = 2
WARM_ROUNDS = 3

FLOPS = 2 * B * MP * MID + 2 * B * MID * HALF


def tile_additivecoupling_pa_kernel(tc, x, h_prev, w_hid, b_hid, w_out, b_out, out):
    nc = tc.nc
    with ExitStack() as ctx:
        keep = ctx.enter_context(tc.tile_pool(name="keep", bufs=1))
        y_pool = ctx.enter_context(tc.tile_pool(name="y_pool", bufs=12))
        psum_acc = ctx.enter_context(tc.psum_pool(name="psum_acc", bufs=4))
        psum_y = ctx.enter_context(tc.psum_pool(name="psum_y", bufs=1))

        hp_rows = keep.tile([P, B_TILES, MP], BF16)
        hp_grouped = [
            keep.tile([P, PASSES, B_HALF * PACK], BF16, align_bytes=64, name="hp_grouped%d" % bh) for bh in range(2)
        ]
        hp_codes = keep.tile([P, PASSES, B], U32, align_bytes=64)
        hp_scales = keep.tile([P, PASSES, B], U8, align_bytes=64)

        w_raw = keep.tile([P, 2, PASSES, PACK, 512], BF16)
        w_grouped = keep.tile([P, 2, PASSES, 512 * PACK], BF16, align_bytes=64)
        w_codes = keep.tile([P, PASSES, MID], U32, align_bytes=64)
        w_scales = keep.tile([P, PASSES, MID], U8, align_bytes=64)

        h_rows = [
            [keep.tile([P, PACK, B_HALF], BF16, name="h_rows%d%d" % (mh, bh)) for bh in range(2)] for mh in range(2)
        ]
        h_grouped = keep.tile([P, PASSES, B * PACK], BF16, align_bytes=64)
        h_codes = keep.tile([P, PASSES, B], U32, align_bytes=64)
        h_scales = keep.tile([P, PASSES, B], U8, align_bytes=64)

        wo_raw = keep.tile([P, PASSES, PACK, HALF], BF16)
        wo_grouped = keep.tile([P, PASSES * HALF * PACK], BF16, align_bytes=64)
        wo_codes = keep.tile([P, PASSES * HALF], U32, align_bytes=64)
        wo_scales = keep.tile([P, PASSES * HALF], U8, align_bytes=64)

        x_rows = keep.tile([P, B_TILES, D], BF16)
        shift_t = keep.tile([P, J_TILES, B], F32)

        ident_f32 = keep.tile([P, P], F32)
        ident_bf16 = keep.tile([P, P], BF16)
        zeros = keep.tile([P, 4 * P], BF16)
        bias_rows = keep.tile([P, PACK * P], BF16)
        bias_cols = keep.tile([P, PACK + 1, PASSES + J_TILES], F32)

        add_banks = [psum_y.tile([P, 4, P], F32, name="add_bank%d" % i) for i in range(ADD_BANKS)]
        merge_banks = [psum_y.tile([P, 2, 2, P], F32, name="merge_bank%d" % i) for i in range(MERGE_BANKS)]

        nc.vector.memset(zeros[:], 0.0)
        nc.vector.memset(bias_rows[:], 0.0)
        nc.scalar.dma_start(out=bias_rows[0:PASSES, :], in_=b_hid.rearrange("(m c) -> m c", m=PASSES))
        nc.scalar.dma_start(
            out=bias_rows[PASSES : PASSES + J_TILES, 0:P], in_=b_out.rearrange("(m p) -> m p", p=P)
        )

        def load_h_prev(duo):
            nc.sync.dma_start(
                out=hp_rows[:, 2 * duo : 2 * duo + 2, :],
                in_=h_prev[2 * P * duo : 2 * P * (duo + 1), :].rearrange("(p k) c -> p k c", k=2),
            )

        def load_w_hid(mh):
            for g in range(PASSES):
                nc.sync.dma_start(
                    out=w_raw[:, mh, g, :, :],
                    in_=w_hid[K_PASS * g : K_PASS * (g + 1), 512 * mh : 512 * mh + 512].rearrange(
                        "(p t) c -> p t c", t=PACK
                    ),
                )

        load_w_hid(0)
        for duo in range(4):
            load_h_prev(duo)
        load_w_hid(1)
        nc.sync.dma_start(
            out=wo_raw[:].rearrange("p g t n -> p g (t n)"),
            in_=w_out.rearrange("(g p t) n -> p g (t n)", p=P, t=PACK),
        )
        for xh in range(2):
            nc.sync.dma_start(
                out=x_rows[:, 4 * xh : 4 * xh + 4, :].rearrange("p (c k) d -> p c (k d)", k=2),
                in_=x[B_HALF * xh : B_HALF * (xh + 1), :].rearrange("(c p k) d -> p c (k d)", p=P, k=2),
            )

        make_identity(nc, ident_f32[:])
        nc.vector.tensor_copy(out=ident_bf16[:], in_=ident_f32[:])

        def spread_biases():
            bias_t = psum_acc.tile([P, PACK + 1, P], BF16, tag="acc")
            for t in range(PACK):
                nc.tensor.transpose(bias_t[:, t, :], bias_rows[:, t : PACK * P : PACK], ident_bf16[:])
            nc.tensor.transpose(bias_t[:, PACK, :], bias_rows[:, 0:P], ident_bf16[:])
            nc.scalar.copy(out=bias_cols[:], in_=bias_t[:, :, 0 : PASSES + J_TILES])

        def zero_add_banks():
            for r in range(WARM_ROUNDS):
                for bank in add_banks:
                    nc.tensor.matmul(
                        bank[:].rearrange("p k j -> p (k j)"),
                        zeros[:, 0:P],
                        zeros[:],
                        start=(r == 0),
                        stop=(r == WARM_ROUNDS - 1),
                    )

        def transpose_h_prev(bt, copy=nc.scalar.copy):
            words = hp_rows[:, bt, :].bitcast(F32)
            pairs_t = psum_acc.tile([P, 2 * PASSES, P], F32, tag="acc")
            for g in range(PASSES):
                for u in range(2):
                    nc.tensor.transpose(
                        pairs_t[:, 2 * g + u, :], words[:, 2 * P * g + u : 2 * P * (g + 1) : 2], ident_f32[:]
                    )
            b0 = (bt % 4) * P * PACK
            copy(
                out=hp_grouped[bt // 4][:, :, b0 : b0 + P * PACK]
                .bitcast(F32)
                .rearrange("q g (b u) -> q g b u", u=2),
                in_=pairs_t[:].rearrange("q (g u) b -> q g b u", u=2),
            )

        def quantise_h_prev(bh):
            cols = slice(bh * B_HALF, (bh + 1) * B_HALF)
            for g in range(PASSES):
                nc.vector.quantize_mx(
                    out=hp_codes[:, g, cols].bitcast(FP8X4), scales=hp_scales[:, g, cols], in_=hp_grouped[bh][:, g, :]
                )

        def regroup(copy, dst, src):
            copy(
                out=dst.rearrange("p (c i) t -> p c t i", i=4),
                in_=src.rearrange("p t (c i) -> p c t i", i=4),
            )

        def regroup_w_hid(mh, g, parts=1):
            n = PACK // parts
            for part in range(parts):
                for_t = slice(n * part, n * (part + 1))
                nc.vector.tensor_copy(
                    out=w_grouped[:, mh, g, :].rearrange("p (t m i j) -> p m t j i", t=PACK, i=2, j=PACK)[
                        :, :, for_t, :, :
                    ],
                    in_=w_raw[:, mh, g, :, :].rearrange("p j (m i t) -> p m t j i", t=PACK, i=2)[:, :, for_t, :, :],
                )

        def quantise_w_hid(mh, g):
            cols = slice(512 * mh, 512 * (mh + 1))
            nc.vector.quantize_mx(
                out=w_codes[:, g, cols].bitcast(FP8X4), scales=w_scales[:, g, cols], in_=w_grouped[:, mh, g, :]
            )

        def hidden_matmuls(mh, bh):
            cols = slice(bh * B_HALF, (bh + 1) * B_HALF)
            for t in range(PACK):
                mt = PACK * mh + t
                acc = psum_acc.tile([P, B_HALF], F32, tag="acc")
                for g in range(PASSES):
                    nc.tensor.matmul_mx(
                        out=acc[:],
                        lhsT=w_codes[:, g, mt * P : (mt + 1) * P].bitcast(FP8X4),
                        lhsT_scale=w_scales[:, g, mt * P : (mt + 1) * P],
                        rhs=hp_codes[:, g, cols].bitcast(FP8X4),
                        rhs_scale=hp_scales[:, g, cols],
                        start=(g == 0),
                        stop=(g == PASSES - 1),
                    )
                nc.scalar.activation(
                    out=h_rows[mh][bh][:, t, :], in_=acc[:], func=RELU, bias=bias_cols[:, t, mh : mh + 1], scale=1.0
                )

        def regroup_hidden(mh, bh):
            wide = slice(bh * B_HALF * PACK, (bh + 1) * B_HALF * PACK)
            regroup(
                nc.vector.tensor_copy,
                h_grouped[:, mh, wide].rearrange("p (c t) -> p c t", t=PACK),
                h_rows[mh][bh][:],
            )

        def quantise_hidden(mh, bh):
            cols = slice(bh * B_HALF, (bh + 1) * B_HALF)
            wide = slice(bh * B_HALF * PACK, (bh + 1) * B_HALF * PACK)
            nc.vector.quantize_mx(
                out=h_codes[:, mh, cols].bitcast(FP8X4), scales=h_scales[:, mh, cols], in_=h_grouped[:, mh, wide]
            )

        def regroup_w_out(copy, g):
            regroup(
                copy,
                wo_grouped[:, g * HALF * PACK : (g + 1) * HALF * PACK].rearrange("p (c t) -> p c t", t=PACK),
                wo_raw[:, g, :, :],
            )

        def quantise_w_out(c0, c1):
            nc.vector.quantize_mx(
                out=wo_codes[:, c0:c1].bitcast(FP8X4),
                scales=wo_scales[:, c0:c1],
                in_=wo_grouped[:, c0 * PACK : c1 * PACK],
            )

        def shift_pass(acc, jt, bh, g):
            cols = slice(bh * B_HALF, (bh + 1) * B_HALF)
            w0 = g * HALF + jt * P
            nc.tensor.matmul_mx(
                out=acc[:],
                lhsT=wo_codes[:, w0 : w0 + P].bitcast(FP8X4),
                lhsT_scale=wo_scales[:, w0 : w0 + P],
                rhs=h_codes[:, g, cols].bitcast(FP8X4),
                rhs_scale=h_scales[:, g, cols],
                start=(g == 0),
                stop=(g == PASSES - 1),
            )

        def open_shift(jt, bh):
            acc = psum_acc.tile([P, B_HALF], F32, tag="acc", name="shift_acc%d" % jt)
            shift_pass(acc, jt, bh, 0)
            return acc

        def close_shift(acc, jt, bh):
            cols = slice(bh * B_HALF, (bh + 1) * B_HALF)
            shift_pass(acc, jt, bh, 1)
            nc.scalar.activation(
                out=shift_t[:, jt, cols],
                in_=acc[:],
                func=IDENTITY,
                bias=bias_cols[:, PACK, PASSES + jt : PASSES + jt + 1],
                scale=1.0,
            )

        def y_columns(jt):
            return slice(2 * P * jt, 2 * P * (jt + 1))

        def store_y(bt, jt, y):
            nc.sync.dma_start(
                out=out[bt * P : (bt + 2) * P, y_columns(jt)].rearrange("(p k) c -> p k c", k=2), in_=y[:]
            )

        def turn_back(bank, bt, jt):
            for k in range(2):
                nc.tensor.transpose(
                    bank[:, 2 * k + 1, :], shift_t[:, jt, (bt + k) * P : (bt + k + 1) * P], ident_f32[:]
                )

        def add_on_vector(bank, bt, jt):
            y = y_pool.tile([P, 2, 2 * P], F32)
            nc.vector.tensor_tensor(
                out=y[:].rearrange("p k (j e) -> p k j e", e=2),
                in0=bank[:].rearrange("p (k e) j -> p k j e", e=2),
                in1=x_rows[:, bt : bt + 2, y_columns(jt)].rearrange("p k (j e) -> p k j e", e=2),
                op=ADD,
            )
            store_y(bt, jt, y)

        def merge_x(bank, bt, jt):
            nc.tensor.matmul(
                bank[:],
                ident_bf16[:],
                x_rows[:, bt : bt + 2, y_columns(jt)].rearrange("p k (j e) -> p k e j", e=2),
                start=True,
                stop=False,
            )

        def merge_shift(bank, bt, jt):
            for k in range(2):
                nc.tensor.matmul(
                    bank[:, k, 1, :],
                    shift_t[:, jt, (bt + k) * P : (bt + k + 1) * P],
                    ident_f32[:],
                    start=False,
                    stop=(k == 1),
                )

        def copy_on_scalar(bank, bt, jt):
            y = y_pool.tile([P, 2, 2 * P], F32)
            nc.scalar.copy(
                out=y[:].rearrange("p k (j e) -> p k j e", e=2), in_=bank[:].rearrange("p k e j -> p k j e")
            )
            store_y(bt, jt, y)

        with tc.manual_schedule():
            vector, scalar = nc.vector.tensor_copy, nc.scalar.copy
            zero_add_banks()
            for g in range(PASSES):
                regroup_w_hid(0, g, parts=2)
            for g in range(PASSES):
                quantise_w_hid(0, g)
            for bt in range(4):
                transpose_h_prev(bt, vector if bt % 2 else scalar)
            quantise_h_prev(0)
            for bt in range(4, 8):
                transpose_h_prev(bt)
            spread_biases()
            hidden_matmuls(0, 0)
            regroup_w_out(scalar, 1)
            regroup_w_hid(1, 0)
            quantise_h_prev(1)
            hidden_matmuls(0, 1)
            regroup_w_hid(1, 1)
            for g in range(PASSES):
                quantise_w_hid(1, g)
            regroup_hidden(0, 0)
            hidden_matmuls(1, 0)
            regroup_w_out(vector, 0)
            quantise_hidden(0, 0)
            regroup_hidden(0, 1)
            hidden_matmuls(1, 1)
            quantise_w_out(0, 512)
            regroup_hidden(1, 0)
            quantise_w_out(512, PASSES * HALF)
            quantise_hidden(1, 0)
            quantise_hidden(0, 1)
            for jt in range(2):
                merge_x(merge_banks[jt], 2, jt)
            shift_0 = [open_shift(jt, 0) for jt in range(J_TILES)]
            for jt in range(J_TILES):
                close_shift(shift_0[jt], jt, 0)
            regroup_hidden(1, 1)
            turn_back(add_banks[0], 0, 0)
            add_on_vector(add_banks[0], 0, 0)
            merge_shift(merge_banks[0], 2, 0)
            copy_on_scalar(merge_banks[0], 2, 0)
            quantise_hidden(1, 1)
            turn_back(add_banks[1], 0, 1)
            add_on_vector(add_banks[1], 0, 1)
            merge_shift(merge_banks[1], 2, 1)
            copy_on_scalar(merge_banks[1], 2, 1)
            close_shift(open_shift(0, 1), 0, 1)
            turn_back(add_banks[0], 0, 2)
            add_on_vector(add_banks[0], 0, 2)
            close_shift(open_shift(1, 1), 1, 1)
            turn_back(add_banks[1], 2, 2)
            add_on_vector(add_banks[1], 2, 2)
            close_shift(open_shift(2, 1), 2, 1)
            merge_x(merge_banks[0], 6, 0)
            turn_back(add_banks[0], 4, 0)
            add_on_vector(add_banks[0], 4, 0)
            merge_shift(merge_banks[0], 6, 0)
            copy_on_scalar(merge_banks[0], 6, 0)
            turn_back(add_banks[1], 4, 1)
            add_on_vector(add_banks[1], 4, 1)
            merge_x(merge_banks[1], 6, 1)
            turn_back(add_banks[0], 4, 2)
            add_on_vector(add_banks[0], 4, 2)
            merge_shift(merge_banks[1], 6, 1)
            copy_on_scalar(merge_banks[1], 6, 1)
            turn_back(add_banks[1], 6, 2)
            add_on_vector(add_banks[1], 6, 2)
